import numpy as np
import ml_dtypes


def mxq(x, axis, fmt="e4m3"):
    dtype, down = {"e4m3": (ml_dtypes.float8_e4m3fn, 7), "e5m2": (ml_dtypes.float8_e5m2, 14)}[fmt]
    v = np.moveaxis(np.asarray(x, np.float32).astype(ml_dtypes.bfloat16).astype(np.float64), axis, -1)
    blocks = v.reshape(v.shape[:-1] + (-1, 32))
    amax = np.abs(blocks).max(-1, keepdims=True)
    byte = np.maximum(np.where(amax > 0, np.frexp(amax)[1] - 1 + 127, 0) - down, 1)
    scale = np.exp2(byte - 127.0)
    codes = (blocks / scale).astype(np.float32).astype(dtype).astype(np.float64)
    return np.moveaxis((codes * scale).reshape(v.shape), -1, axis)


WIDE = False


def mx_kscale(k):
    if not WIDE:
        return np.ones(k)
    levels = np.array([30, -30])
    if k % 512:
        return np.exp2(np.random.permutation(np.resize(levels, k // 32))).repeat(32)
    a = np.empty((k // 512, 16))
    for p in range(k // 512):
        a[p, :8] = np.random.permutation(np.resize(levels, 8))
        for g in range(8):
            far = levels[np.abs(levels - a[p, g]) >= 10]
            a[p, g + 8] = far[np.random.randint(len(far))]
    return np.exp2(a.ravel()).repeat(32)


BF16 = ml_dtypes.bfloat16


def bf(x):
    return np.asarray(x, np.float32).astype(BF16)


def f64(x):
    return np.asarray(x).astype(np.float64)


E2M1 = np.array([0.0, 0.5, 1.0, 1.5, 2.0, 3.0, 4.0, 6.0, -0.0, -0.5, -1.0, -1.5, -2.0, -3.0, -4.0, -6.0])


def pack_weight(w, fmt):
    k, n = w.shape
    w = f64(bf(w)).reshape(k // 32, 32, n)
    amax = np.abs(w).max(1)
    if fmt == "e4m3":
        byte = np.frexp(amax)[1] - 1 + 127 - 7
    else:
        mant, ex = np.frexp(amax / 6.0)
        byte = np.where(mant > 0.5, ex, ex - 1) + 127
    byte = np.clip(np.where(amax > 0, byte, 1), 1, 254)
    scaled = (w * np.exp2(127.0 - byte)[:, None, :]).reshape(k, n).astype(np.float32)
    by_word = np.ascontiguousarray(scaled.reshape(k // 512, 128, 4, n).transpose(0, 1, 3, 2))
    if fmt == "e4m3":
        words = by_word.astype(ml_dtypes.float8_e4m3fn).view(np.uint8)
    else:
        c = by_word.astype(ml_dtypes.float4_e2m1fn).view(np.uint8) & 0xF
        words = c[..., 0::2] | (c[..., 1::2] << 4)
    return np.ascontiguousarray(words), np.ascontiguousarray(byte.astype(np.uint8).reshape(k // 512, 16, n))


def unpack_weight(words, scales, fmt):
    g, p, n, _ = words.shape
    if fmt == "e4m3":
        vals = np.ascontiguousarray(words).view(ml_dtypes.float8_e4m3fn).astype(np.float64)
    else:
        nib = np.empty((g, p, n, 4), np.uint8)
        nib[..., 0::2] = words & 0xF
        nib[..., 1::2] = words >> 4
        vals = E2M1[nib]
    vals = vals * np.repeat(np.exp2(scales.astype(np.float64) - 127.0), 8, axis=1)[..., None]
    return vals.transpose(0, 1, 3, 2).reshape(g * 512, n)

def pack4(w):
    words, scales = pack_weight(w, "e2m1")
    return words.reshape(words.shape[0], 128, -1), scales


def unpack4(words, scales):
    return unpack_weight(words.reshape(words.shape[0], 128, -1, 2), scales, "e2m1")


B, S, H, NH, HD = 2, 256, 2048, 16, 128
BASE = 10000.0


def rope_tables():
    inv_freq = 1.0 / BASE ** (np.arange(0, HD, 2) / HD)
    freqs = np.arange(S)[:, None] * inv_freq[None, :]
    emb = np.concatenate([freqs, freqs], axis=-1)
    return np.cos(emb), np.sin(emb)


def rotate_half(u):
    u1, u2 = np.split(u, 2, axis=-1)
    return np.concatenate([-u2, u1], axis=-1)


def setup_inputs():
    s = mx_kscale(H)
    hidden_states = bf(np.random.standard_normal((B, S, H)) * s)
    wq = np.random.standard_normal((NH * HD, H)) / np.sqrt(H) / s[None, :]
    wk = np.random.standard_normal((NH * HD, H)) / np.sqrt(H) / s[None, :]
    wq_words, wq_scales = pack4(np.ascontiguousarray(wq.T))
    wk_words, wk_scales = pack4(np.ascontiguousarray(wk.T))
    return {"hidden_states": hidden_states,
            "Wq_words": wq_words, "Wq_scales": wq_scales,
            "Wk_words": wk_words, "Wk_scales": wk_scales}


def reference(hidden_states, Wq_words, Wq_scales, Wk_words, Wk_scales):
    xq = mxq(f64(hidden_states), 2, "e5m2")
    q = xq @ unpack4(Wq_words, Wq_scales)
    k = xq @ unpack4(Wk_words, Wk_scales)
    q = q.reshape(B, S, NH, HD).transpose(0, 2, 1, 3)
    k = k.reshape(B, S, NH, HD).transpose(0, 2, 1, 3)
    cos, sin = rope_tables()
    cos = cos[None, None]
    sin = sin[None, None]
    q_rot = q * cos + rotate_half(q) * sin
    k_rot = k * cos + rotate_half(k) * sin
    return q_rot, k_rot

@@ -1,0 +1,201 @@
+from contextlib import ExitStack
+import math
+
+import concourse.mybir as mybir
+from concourse.masks import make_identity
+
+F32 = mybir.dt.float32
+BF16 = mybir.dt.bfloat16
+I32 = mybir.dt.int32
+U32 = mybir.dt.uint32
+U8 = mybir.dt.uint8
+E5X4 = mybir.dt.float8_e5m2_x4
+E2X4 = mybir.dt.float4_e2m1fn_x4
+ALU = mybir.AluOpType
+ACT = mybir.ActivationFunctionType
+
+FLOPS = 2 * 512 * 2048 * 4096
+
+P = 128
+PASSES = 4
+RATIO = 10000.0 ** (-1.0 / 64.0)
+TWO_PI_HI = 6.28125
+TWO_PI_LO = 2.0 * math.pi - TWO_PI_HI
+W_LOADS = ((0, 0, 1), (0, 1, 1), (0, 2, 2), (1, 0, 2), (1, 2, 2))
+
+
+def tile_multiheadattention_pa_kernel(tc, hidden_states, Wq_words, Wq_scales, Wk_words, Wk_scales, out_0, out_1):
+    nc = tc.nc
+    w_words = (Wq_words, Wk_words)
+    w_scales = (Wq_scales, Wk_scales)
+    outs = (out_0, out_1)
+
+    with ExitStack() as ctx:
+        keep = ctx.enter_context(tc.tile_pool(name="keep", bufs=1))
+        work = ctx.enter_context(tc.tile_pool(name="work", bufs=3))
+        psum = ctx.enter_context(tc.psum_pool(name="psum", bufs=8))
+
+        x_sb = []
+        for t in range(4):
+            x_t = keep.tile([P, 2048], BF16, name="x%d" % t)
+            x_sb.append(x_t)
+
+        def load_x(t, pieces):
+            b, e = divmod(t, 2)
+            src = hidden_states[b].rearrange("(m e) k -> m e k", e=2)
+            step = 2048 // pieces
+            for i in range(pieces):
+                nc.sync.dma_start(out=x_sb[t][:, i * step:(i + 1) * step], in_=src[:, e, i * step:(i + 1) * step])
+
+        words = {}
+        planes = {}
+
+        def load_w(i):
+            mat, first, count = W_LOADS[i]
+            wt = keep.tile([P, PASSES, 1024 * count], U8, name="w%d" % i, align_bytes=64)
+            pl = keep.tile([P, PASSES, 512 * count], U8, name="s%d" % i, align_bytes=64)
+            nc.vector.memset(pl[:].bitcast(I32), 0)
+            c0 = 512 * first
+            c1 = c0 + 512 * count
+            for q in range(4):
+                nc.sync.dma_start(
+                    out=pl[32 * q:32 * q + 4, :, :].bitcast(I32),
+                    in_=w_scales[mat][:, 4 * q:4 * q + 4, c0:c1].rearrange("g r n -> r g n").bitcast(I32),
+                )
+            nc.sync.dma_start(
+                out=wt[:].bitcast(I32),
+                in_=w_words[mat][:, :, 2 * c0:2 * c1].rearrange("g p n -> p g n").bitcast(I32),
+            )
+            for j in range(count):
+                words[(mat, first + j)] = (wt, j)
+                planes[(mat, first + j)] = (pl, j)
+
+        warm = keep.tile([P, 1], F32, name="warm")
+        nc.vector.memset(warm[:], 0.0)
+        nc.scalar.activation(out=warm[:], in_=warm[:], func=ACT.Sin)
+
+        load_x(0, 2)
+        load_w(0)
+        load_x(1, 1)
+        load_x(2, 1)
+        load_x(3, 1)
+        for i in range(1, len(W_LOADS)):
+            load_w(i)
+
+        ident = keep.tile([P, P], F32, name="ident")
+        make_identity(nc, ident[:])
+
+        ang = keep.tile([P, 2, 64], F32, name="ang")
+        nc.gpsimd.iota(ang[:, :, 0:1], pattern=[[1, 2]], base=0, channel_multiplier=2, allow_small_or_imprecise_dtypes=True)
+        for s in range(6):
+            w = 1 << s
+            nc.gpsimd.tensor_scalar(out=ang[:, :, w:2 * w], in0=ang[:, :, 0:w], scalar1=RATIO ** w, scalar2=0.0, op0=ALU.mult, op1=ALU.add)
+        turns = keep.tile([P, 2, 64], I32, name="turns")
+        nc.vector.tensor_scalar(out=turns[:], in0=ang[:], scalar1=1.0 / (2.0 * math.pi), scalar2=0.25, op0=ALU.mult, op1=ALU.add)
+        red1 = keep.tile([P, 2, 64], F32, name="red1")
+        nc.vector.scalar_tensor_tensor(out=red1[:], in0=turns[:], scalar=-TWO_PI_HI, in1=ang[:], op0=ALU.mult, op1=ALU.add)
+        red = keep.tile([P, 2, 64], F32, name="red")
+        nc.vector.scalar_tensor_tensor(out=red[:], in0=turns[:], scalar=-TWO_PI_LO, in1=red1[:], op0=ALU.mult, op1=ALU.add)
+        sin_half = keep.tile([P, 2, 64], F32, name="sin_half")
+        nc.scalar.activation(out=sin_half[:], in_=red[:], func=ACT.Sin, scale=0.5)
+        sin_quarter = keep.tile([P, 2, 64], F32, name="sin_quarter")
+        nc.scalar.activation(out=sin_quarter[:], in_=red[:], func=ACT.Sin, scale=0.25)
+
+        tab = keep.tile([P, 2, 256], F32, name="tab")
+        tab_k = tab[:].rearrange("p e (k j) -> p e k j", k=4)
+
+        def finish_tables():
+            hh = keep.tile([P, 2, 64], F32, name="hh")
+            nc.gpsimd.tensor_tensor(out=hh[:], in0=sin_half[:], in1=sin_half[:], op=ALU.mult)
+            nc.gpsimd.tensor_scalar(out=tab_k[:, :, 0:4:3, :], in0=hh[:].unsqueeze(2).to_broadcast([P, 2, 2, 64]), scalar1=-2.0, scalar2=1.0, op0=ALU.mult, op1=ALU.add)
+            qq = keep.tile([P, 2, 64], F32, name="qq")
+            nc.gpsimd.tensor_tensor(out=qq[:], in0=sin_quarter[:], in1=sin_quarter[:], op=ALU.mult)
+            cos_half = keep.tile([P, 2, 64], F32, name="cos_half")
+            nc.gpsimd.tensor_scalar(out=cos_half[:], in0=qq[:], scalar1=-2.0, scalar2=1.0, op0=ALU.mult, op1=ALU.add)
+            hc = keep.tile([P, 2, 64], F32, name="hc")
+            nc.gpsimd.tensor_tensor(out=hc[:], in0=sin_half[:], in1=cos_half[:], op=ALU.mult)
+            nc.gpsimd.tensor_scalar(out=tab_k[:, :, 2, :], in0=hc[:], scalar1=2.0, scalar2=0.0, op0=ALU.mult, op1=ALU.add)
+            nc.gpsimd.tensor_scalar(out=tab_k[:, :, 1, :], in0=hc[:], scalar1=-2.0, scalar2=0.0, op0=ALU.mult, op1=ALU.add)
+
+        codes = []
+        x_scales = []
+        grouped = []
+        for t in range(4):
+            c_t = keep.tile([P, PASSES, P], U32, name="codes%d" % t, align_bytes=64)
+            s_t = keep.tile([P, PASSES, P], U8, name="xs%d" % t, align_bytes=64)
+            g_t = keep.tile([P, PASSES, P, 4], BF16, name="grp%d" % t, align_bytes=64)
+            codes.append(c_t)
+            x_scales.append(s_t)
+            grouped.append(g_t)
+
+        def prepare_x(t):
+            x_words = x_sb[t][:].bitcast(F32)
+            g32 = grouped[t][:].rearrange("p g r t -> p g (r t)").bitcast(F32).rearrange("p g (r u) -> p g r u", u=2)
+            for hb in range(2):
+                xt = psum.tile([P, 2, 2, P], F32, tag="bank", name="xt")
+                for gi in range(2):
+                    g = 2 * hb + gi
+                    for u in range(2):
+                        nc.tensor.transpose(xt[:, gi, u, :], x_words[:, 256 * g + u:256 * (g + 1):2], ident[:])
+                nc.scalar.copy(out=g32[:, 2 * hb:2 * hb + 2, :, :], in_=xt[:].rearrange("p g u r -> p g r u"))
+                nc.vector.quantize_mx(
+                    out=codes[t][:, 2 * hb:2 * hb + 2, :].rearrange("p g m -> p (g m)").bitcast(E5X4),
+                    scales=x_scales[t][:, 2 * hb:2 * hb + 2, :].rearrange("p g m -> p (g m)"),
+                    in_=grouped[t][:, 2 * hb:2 * hb + 2, :, :].rearrange("p g r t -> p (g r t)"),
+                )
+
+        p_tiles = {}
+
+        def project(mat, blk, t, on_vector=False):
+            b, e = divmod(t, 2)
+            wt, j = words[(mat, blk)]
+            pl, j = planes[(mat, blk)]
+            acc = psum.tile([P, 512], F32, tag="bank", name="acc")
+            for g in range(PASSES):
+                nc.tensor.matmul_mx(
+                    out=acc[:],
+                    lhsT=codes[t][:, g, :].bitcast(E5X4),
+                    lhsT_scale=x_scales[t][:, g, :],
+                    rhs=wt[:, g, 1024 * j:1024 * (j + 1)].bitcast(E2X4),
+                    rhs_scale=pl[:, g, 512 * j:512 * (j + 1)],
+                    start=(g == 0),
+                    stop=(g == PASSES - 1),
+                )
+            if e == 0:
+                p_new = work.tile([P, 4, 2, 2, P], F32, name="p_new")
+                p_tiles[b] = p_new
+            prod = p_tiles[b]
+            nc.vector.tensor_tensor(
+                out=prod[:, :, e, :, :].rearrange("p h w d -> p w h d"),
+                in0=acc[:].rearrange("p (h d) -> p h d", h=4).unsqueeze(1).to_broadcast([P, 2, 4, P]),
+                in1=tab[:, e, :].rearrange("p (w d) -> p w d", w=2).unsqueeze(2).to_broadcast([P, 2, 4, P]),
+                op=ALU.mult,
+            )
+            if e == 1:
+                o_t = work.tile([P, 4, 2, P], F32, name="o_t")
+                pv = prod[:].rearrange("p h e w (u j) -> p (h e w) u j", u=2)
+                adder = nc.vector if on_vector else nc.gpsimd
+                adder.tensor_tensor(
+                    out=o_t[:].rearrange("p h e (w j) -> p (h e w) j", w=2),
+                    in0=pv[:, :, 0, :],
+                    in1=pv[:, :, 1, :],
+                    op=ALU.add,
+                )
+                nc.scalar.dma_start(
+                    out=outs[mat][b, 4 * blk:4 * blk + 4].rearrange("h (m e) d -> m h (e d)", e=2),
+                    in_=o_t[:].rearrange("p h e d -> p h (e d)"),
+                )
+
+        prepare_x(0)
+        prepare_x(1)
+        finish_tables()
+        project(0, 0, 0)
+        prepare_x(2)
+        project(0, 0, 1)
+        prepare_x(3)
+        project(0, 0, 2)
+        project(0, 0, 3)
+        for c in range(1, 8):
+            mat, blk = divmod(c, 4)
+            for t in range(4):
+                project(mat, blk, t, on_vector=(c == 7 and t >= 2))

@@ -70,52 +70,41 @@ def tile_multiheadattention_pa_kernel(tc, hidden_states, Wq_words, Wq_scales, Wk
                 words[(mat, first + j)] = (wt, j)
                 planes[(mat, first + j)] = (pl, j)
 
+        ang = keep.tile([P, 2, 64], F32, name="ang")
+        nc.gpsimd.iota(ang[:, :, 0:1], pattern=[[1, 2]], base=0, channel_multiplier=2, allow_small_or_imprecise_dtypes=True)
+        ident = keep.tile([P, P], F32, name="ident")
+        make_identity(nc, ident[:])
+
         warm = keep.tile([P, 1], F32, name="warm")
         nc.vector.memset(warm[:], 0.0)
         nc.scalar.activation(out=warm[:], in_=warm[:], func=ACT.Sin)
 
         load_x(0, 2)
         load_w(0)
+
+        for s in range(6):
+            w = 1 << s
+            nc.vector.tensor_scalar(out=ang[:, :, w:2 * w], in0=ang[:, :, 0:w], scalar1=RATIO ** w, scalar2=None, op0=ALU.mult)
+        turns = keep.tile([P, 2, 64], I32, name="turns")
+        nc.vector.tensor_scalar(out=turns[:], in0=ang[:], scalar1=1.0 / (2.0 * math.pi), scalar2=None, op0=ALU.mult)
+        red1 = keep.tile([P, 2, 64], F32, name="red1")
+        nc.vector.scalar_tensor_tensor(out=red1[:], in0=turns[:], scalar=-TWO_PI_HI, in1=ang[:], op0=ALU.mult, op1=ALU.add)
+        red = keep.tile([P, 2, 64], F32, name="red")
+        nc.vector.scalar_tensor_tensor(out=red[:], in0=turns[:], scalar=-TWO_PI_LO, in1=red1[:], op0=ALU.mult, op1=ALU.add)
+        absred = keep.tile([P, 2, 64], F32, name="absred")
+        nc.vector.scalar_tensor_tensor(out=absred[:], in0=red[:], scalar=-1.0, in1=red[:], op0=ALU.mult, op1=ALU.max)
+
+        tab = keep.tile([P, 2, 256], F32, name="tab")
+        tab_k = tab[:].rearrange("p e (k j) -> p e k j", k=4)
+        nc.scalar.activation(out=tab_k[:, :, 2, :], in_=red[:], func=ACT.Sin)
+        nc.scalar.activation(out=tab_k[:, :, 1, :], in_=red[:], func=ACT.Sin, scale=-1.0)
+        nc.scalar.activation(out=tab_k[:, :, 0:4:3, :], in_=absred[:].unsqueeze(2).to_broadcast([P, 2, 2, 64]), func=ACT.Sin, scale=-1.0, bias=0.5 * math.pi)
+
         load_x(1, 1)
         load_x(2, 1)
         load_x(3, 1)
         for i in range(1, len(W_LOADS)):
             load_w(i)
-
-        ident = keep.tile([P, P], F32, name="ident")
-        make_identity(nc, ident[:])
-
-        ang = keep.tile([P, 2, 64], F32, name="ang")
-        nc.gpsimd.iota(ang[:, :, 0:1], pattern=[[1, 2]], base=0, channel_multiplier=2, allow_small_or_imprecise_dtypes=True)
-        for s in range(6):
-            w = 1 << s
-            nc.gpsimd.tensor_scalar(out=ang[:, :, w:2 * w], in0=ang[:, :, 0:w], scalar1=RATIO ** w, scalar2=0.0, op0=ALU.mult, op1=ALU.add)
-        turns = keep.tile([P, 2, 64], I32, name="turns")
-        nc.vector.tensor_scalar(out=turns[:], in0=ang[:], scalar1=1.0 / (2.0 * math.pi), scalar2=0.25, op0=ALU.mult, op1=ALU.add)
-        red1 = keep.tile([P, 2, 64], F32, name="red1")
-        nc.vector.scalar_tensor_tensor(out=red1[:], in0=turns[:], scalar=-TWO_PI_HI, in1=ang[:], op0=ALU.mult, op1=ALU.add)
-        red = keep.tile([P, 2, 64], F32, name="red")
-        nc.vector.scalar_tensor_tensor(out=red[:], in0=turns[:], scalar=-TWO_PI_LO, in1=red1[:], op0=ALU.mult, op1=ALU.add)
-        sin_half = keep.tile([P, 2, 64], F32, name="sin_half")
-        nc.scalar.activation(out=sin_half[:], in_=red[:], func=ACT.Sin, scale=0.5)
-        sin_quarter = keep.tile([P, 2, 64], F32, name="sin_quarter")
-        nc.scalar.activation(out=sin_quarter[:], in_=red[:], func=ACT.Sin, scale=0.25)
-
-        tab = keep.tile([P, 2, 256], F32, name="tab")
-        tab_k = tab[:].rearrange("p e (k j) -> p e k j", k=4)
-
-        def finish_tables():
-            hh = keep.tile([P, 2, 64], F32, name="hh")
-            nc.gpsimd.tensor_tensor(out=hh[:], in0=sin_half[:], in1=sin_half[:], op=ALU.mult)
-            nc.gpsimd.tensor_scalar(out=tab_k[:, :, 0:4:3, :], in0=hh[:].unsqueeze(2).to_broadcast([P, 2, 2, 64]), scalar1=-2.0, scalar2=1.0, op0=ALU.mult, op1=ALU.add)
-            qq = keep.tile([P, 2, 64], F32, name="qq")
-            nc.gpsimd.tensor_tensor(out=qq[:], in0=sin_quarter[:], in1=sin_quarter[:], op=ALU.mult)
-            cos_half = keep.tile([P, 2, 64], F32, name="cos_half")
-            nc.gpsimd.tensor_scalar(out=cos_half[:], in0=qq[:], scalar1=-2.0, scalar2=1.0, op0=ALU.mult, op1=ALU.add)
-            hc = keep.tile([P, 2, 64], F32, name="hc")
-            nc.gpsimd.tensor_tensor(out=hc[:], in0=sin_half[:], in1=cos_half[:], op=ALU.mult)
-            nc.gpsimd.tensor_scalar(out=tab_k[:, :, 2, :], in0=hc[:], scalar1=2.0, scalar2=0.0, op0=ALU.mult, op1=ALU.add)
-            nc.gpsimd.tensor_scalar(out=tab_k[:, :, 1, :], in0=hc[:], scalar1=-2.0, scalar2=0.0, op0=ALU.mult, op1=ALU.add)
 
         codes = []
         x_scales = []
@@ -188,7 +177,6 @@ def tile_multiheadattention_pa_kernel(tc, hidden_states, Wq_words, Wq_scales, Wk
 
         prepare_x(0)
         prepare_x(1)
-        finish_tables()
         project(0, 0, 0)
         prepare_x(2)
         project(0, 0, 1)

@@ -33,7 +33,8 @@ def tile_multiheadattention_pa_kernel(tc, hidden_states, Wq_words, Wq_scales, Wk
     with ExitStack() as ctx:
         keep = ctx.enter_context(tc.tile_pool(name="keep", bufs=1))
         work = ctx.enter_context(tc.tile_pool(name="work", bufs=3))
-        psum = ctx.enter_context(tc.psum_pool(name="psum", bufs=8))
+        psum = ctx.enter_context(tc.psum_pool(name="psum", bufs=7))
+        psum_idle = ctx.enter_context(tc.psum_pool(name="psum_idle", bufs=1))
 
         x_sb = []
         for t in range(4):
@@ -70,6 +71,14 @@ def tile_multiheadattention_pa_kernel(tc, hidden_states, Wq_words, Wq_scales, Wk
                 words[(mat, first + j)] = (wt, j)
                 planes[(mat, first + j)] = (pl, j)
 
+        zeros = keep.tile([P, 512], BF16, name="zeros")
+        nc.gpsimd.memset(zeros[:], 0.0)
+        idle_bank = psum_idle.tile([P, 512], F32, name="idle_bank")
+
+        def keep_clock(count):
+            for i in range(count):
+                nc.tensor.matmul(out=idle_bank[:], lhsT=zeros[:, 0:P], rhs=zeros[:], start=True, stop=True)
+
         ang = keep.tile([P, 2, 64], F32, name="ang")
         nc.gpsimd.iota(ang[:, :, 0:1], pattern=[[1, 2]], base=0, channel_multiplier=2, allow_small_or_imprecise_dtypes=True)
         ident = keep.tile([P, P], F32, name="ident")
@@ -80,6 +89,9 @@ def tile_multiheadattention_pa_kernel(tc, hidden_states, Wq_words, Wq_scales, Wk
         nc.scalar.activation(out=warm[:], in_=warm[:], func=ACT.Sin)
 
         load_x(0, 2)
+        load_x(1, 1)
+        load_x(2, 1)
+        load_x(3, 1)
         load_w(0)
 
         for s in range(6):
@@ -100,9 +112,6 @@ def tile_multiheadattention_pa_kernel(tc, hidden_states, Wq_words, Wq_scales, Wk
         nc.scalar.activation(out=tab_k[:, :, 1, :], in_=red[:], func=ACT.Sin, scale=-1.0)
         nc.scalar.activation(out=tab_k[:, :, 0:4:3, :], in_=absred[:].unsqueeze(2).to_broadcast([P, 2, 2, 64]), func=ACT.Sin, scale=-1.0, bias=0.5 * math.pi)
 
-        load_x(1, 1)
-        load_x(2, 1)
-        load_x(3, 1)
         for i in range(1, len(W_LOADS)):
             load_w(i)
 
@@ -175,14 +184,19 @@ def tile_multiheadattention_pa_kernel(tc, hidden_states, Wq_words, Wq_scales, Wk
                     in_=o_t[:].rearrange("p h e d -> p h (e d)"),
                 )
 
-        prepare_x(0)
-        prepare_x(1)
-        project(0, 0, 0)
-        prepare_x(2)
-        project(0, 0, 1)
-        prepare_x(3)
-        project(0, 0, 2)
-        project(0, 0, 3)
+        with tc.manual_schedule(engines={mybir.EngineType.PE}):
+            keep_clock(4)
+            prepare_x(0)
+            keep_clock(2)
+            prepare_x(1)
+            keep_clock(2)
+            prepare_x(2)
+            keep_clock(2)
+            prepare_x(3)
+            project(0, 0, 0)
+            project(0, 0, 1)
+            project(0, 0, 2)
+            project(0, 0, 3)
         for c in range(1, 8):
             mat, blk = divmod(c, 4)
             for t in range(4):

@@ -144,7 +144,7 @@ def tile_multiheadattention_pa_kernel(tc, hidden_states, Wq_words, Wq_scales, Wk
 
         p_tiles = {}
 
-        def project(mat, blk, t, on_vector=False):
+        def project(mat, blk, t):
             b, e = divmod(t, 2)
             wt, j = words[(mat, blk)]
             pl, j = planes[(mat, blk)]
@@ -169,20 +169,20 @@ def tile_multiheadattention_pa_kernel(tc, hidden_states, Wq_words, Wq_scales, Wk
                 in1=tab[:, e, :].rearrange("p (w d) -> p w d", w=2).unsqueeze(2).to_broadcast([P, 2, 4, P]),
                 op=ALU.mult,
             )
-            if e == 1:
-                o_t = work.tile([P, 4, 2, P], F32, name="o_t")
-                pv = prod[:].rearrange("p h e w (u j) -> p (h e w) u j", u=2)
-                adder = nc.vector if on_vector else nc.gpsimd
-                adder.tensor_tensor(
-                    out=o_t[:].rearrange("p h e (w j) -> p (h e w) j", w=2),
-                    in0=pv[:, :, 0, :],
-                    in1=pv[:, :, 1, :],
-                    op=ALU.add,
-                )
-                nc.scalar.dma_start(
-                    out=outs[mat][b, 4 * blk:4 * blk + 4].rearrange("h (m e) d -> m h (e d)", e=2),
-                    in_=o_t[:].rearrange("p h e d -> p h (e d)"),
-                )
+
+        def finish(mat, blk, b, adder):
+            o_t = work.tile([P, 4, 2, P], F32, name="o_t")
+            pv = p_tiles[b][:].rearrange("p h e w (u j) -> p (h e w) u j", u=2)
+            adder.tensor_tensor(
+                out=o_t[:].rearrange("p h e (w j) -> p (h e w) j", w=2),
+                in0=pv[:, :, 0, :],
+                in1=pv[:, :, 1, :],
+                op=ALU.add,
+            )
+            nc.scalar.dma_start(
+                out=outs[mat][b, 4 * blk:4 * blk + 4].rearrange("h (m e) d -> m h (e d)", e=2),
+                in_=o_t[:].rearrange("p h e d -> p h (e d)"),
+            )
 
         with tc.manual_schedule(engines={mybir.EngineType.PE}):
             keep_clock(4)
@@ -193,11 +193,17 @@ def tile_multiheadattention_pa_kernel(tc, hidden_states, Wq_words, Wq_scales, Wk
             prepare_x(2)
             keep_clock(2)
             prepare_x(3)
-            project(0, 0, 0)
-            project(0, 0, 1)
-            project(0, 0, 2)
-            project(0, 0, 3)
-        for c in range(1, 8):
+            for b in range(2):
+                project(0, 0, 2 * b)
+                project(0, 0, 2 * b + 1)
+                finish(0, 0, b, nc.gpsimd)
+        for c in range(1, 7):
             mat, blk = divmod(c, 4)
-            for t in range(4):
-                project(mat, blk, t, on_vector=(c == 7 and t >= 2))
+            for b in range(2):
+                project(mat, blk, 2 * b)
+                project(mat, blk, 2 * b + 1)
+                finish(mat, blk, b, nc.gpsimd)
+        for t in range(4):
+            project(1, 3, t)
+        for b in range(2):
+            finish(1, 3, b, nc.vector)

@@ -187,11 +187,9 @@ def tile_multiheadattention_pa_kernel(tc, hidden_states, Wq_words, Wq_scales, Wk
         with tc.manual_schedule(engines={mybir.EngineType.PE}):
             keep_clock(4)
             prepare_x(0)
-            keep_clock(2)
             prepare_x(1)
             keep_clock(2)
             prepare_x(2)
-            keep_clock(2)
             prepare_x(3)
             for b in range(2):
                 project(0, 0, 2 * b)

@@ -33,6 +33,7 @@ def tile_multiheadattention_pa_kernel(tc, hidden_states, Wq_words, Wq_scales, Wk
     with ExitStack() as ctx:
         keep = ctx.enter_context(tc.tile_pool(name="keep", bufs=1))
         work = ctx.enter_context(tc.tile_pool(name="work", bufs=3))
+        products = ctx.enter_context(tc.tile_pool(name="products", bufs=12))
         psum = ctx.enter_context(tc.psum_pool(name="psum", bufs=7))
         psum_idle = ctx.enter_context(tc.psum_pool(name="psum_idle", bufs=1))
 
@@ -160,7 +161,7 @@ def tile_multiheadattention_pa_kernel(tc, hidden_states, Wq_words, Wq_scales, Wk
                     stop=(g == PASSES - 1),
                 )
             if e == 0:
-                p_new = work.tile([P, 4, 2, 2, P], F32, name="p_new")
+                p_new = products.tile([P, 4, 2, 2, P], F32, name="p_new")
                 p_tiles[b] = p_new
             prod = p_tiles[b]
             nc.vector.tensor_tensor(
@@ -170,19 +171,22 @@ def tile_multiheadattention_pa_kernel(tc, hidden_states, Wq_words, Wq_scales, Wk
                 op=ALU.mult,
             )
 
-        def finish(mat, blk, b, adder):
+        def finish(mat, blk, b, adder, pieces=1):
             o_t = work.tile([P, 4, 2, P], F32, name="o_t")
-            pv = p_tiles[b][:].rearrange("p h e w (u j) -> p (h e w) u j", u=2)
-            adder.tensor_tensor(
-                out=o_t[:].rearrange("p h e (w j) -> p (h e w) j", w=2),
-                in0=pv[:, :, 0, :],
-                in1=pv[:, :, 1, :],
-                op=ALU.add,
-            )
-            nc.scalar.dma_start(
-                out=outs[mat][b, 4 * blk:4 * blk + 4].rearrange("h (m e) d -> m h (e d)", e=2),
-                in_=o_t[:].rearrange("p h e d -> p h (e d)"),
-            )
+            heads = 4 // pieces
+            for i in range(pieces):
+                hs = slice(heads * i, heads * (i + 1))
+                pv = p_tiles[b][:, hs].rearrange("p h e w (u j) -> p (h e w) u j", u=2)
+                adder.tensor_tensor(
+                    out=o_t[:, hs].rearrange("p h e (w j) -> p (h e w) j", w=2),
+                    in0=pv[:, :, 0, :],
+                    in1=pv[:, :, 1, :],
+                    op=ALU.add,
+                )
+                nc.scalar.dma_start(
+                    out=outs[mat][b, 4 * blk + heads * i:4 * blk + heads * (i + 1)].rearrange("h (m e) d -> m h (e d)", e=2),
+                    in_=o_t[:, hs].rearrange("p h e d -> p h (e d)"),
+                )
 
         with tc.manual_schedule(engines={mybir.EngineType.PE}):
             keep_clock(4)
@@ -203,5 +207,5 @@ def tile_multiheadattention_pa_kernel(tc, hidden_states, Wq_words, Wq_scales, Wk
                 finish(mat, blk, b, nc.gpsimd)
         for t in range(4):
             project(1, 3, t)
-        for b in range(2):
-            finish(1, 3, b, nc.vector)
+        finish(1, 3, 0, nc.vector)
+        finish(1, 3, 1, nc.vector, pieces=2)

@@ -189,7 +189,7 @@ def tile_multiheadattention_pa_kernel(tc, hidden_states, Wq_words, Wq_scales, Wk
                 )
 
         with tc.manual_schedule(engines={mybir.EngineType.PE}):
-            keep_clock(4)
+            keep_clock(3)
             prepare_x(0)
             prepare_x(1)
             keep_clock(2)

@@ -32,7 +32,7 @@ def tile_multiheadattention_pa_kernel(tc, hidden_states, Wq_words, Wq_scales, Wk
 
     with ExitStack() as ctx:
         keep = ctx.enter_context(tc.tile_pool(name="keep", bufs=1))
-        work = ctx.enter_context(tc.tile_pool(name="work", bufs=3))
+        work = ctx.enter_context(tc.tile_pool(name="work", bufs=5))
         products = ctx.enter_context(tc.tile_pool(name="products", bufs=12))
         psum = ctx.enter_context(tc.psum_pool(name="psum", bufs=7))
         psum_idle = ctx.enter_context(tc.psum_pool(name="psum_idle", bufs=1))
@@ -171,7 +171,7 @@ def tile_multiheadattention_pa_kernel(tc, hidden_states, Wq_words, Wq_scales, Wk
                 op=ALU.mult,
             )
 
-        def finish(mat, blk, b, adder, pieces=1):
+        def finish(mat, blk, b, adder, pieces=1, queue=None):
             o_t = work.tile([P, 4, 2, P], F32, name="o_t")
             heads = 4 // pieces
             for i in range(pieces):
@@ -183,8 +183,23 @@ def tile_multiheadattention_pa_kernel(tc, hidden_states, Wq_words, Wq_scales, Wk
                     in1=pv[:, :, 1, :],
                     op=ALU.add,
                 )
-                nc.scalar.dma_start(
+                (queue or nc.scalar).dma_start(
                     out=outs[mat][b, 4 * blk + heads * i:4 * blk + heads * (i + 1)].rearrange("h (m e) d -> m h (e d)", e=2),
+                    in_=o_t[:, hs].rearrange("p h e d -> p h (e d)"),
+                )
+
+        def finish_on_tensor(mat, blk, b, prod):
+            o_t = work.tile([P, 4, 2, P], F32, name="o_t")
+            pv = prod[:].rearrange("p h e w (u j) -> p h e w u j", u=2)
+            for i in range(2):
+                hs = slice(2 * i, 2 * i + 2)
+                total = psum.tile([P, 2, 2, P], F32, tag="bank", name="total")
+                for e in range(2):
+                    for u in range(2):
+                        nc.tensor.matmul(out=total[:, e, :, :], lhsT=ident[:], rhs=pv[:, hs, e, :, u, :], start=(u == 0), stop=(u == 1))
+                nc.scalar.copy(out=o_t[:, hs, :, :], in_=total[:].rearrange("p e h d -> p h e d"))
+                nc.scalar.dma_start(
+                    out=outs[mat][b, 4 * blk + 2 * i:4 * blk + 2 * i + 2].rearrange("h (m e) d -> m h (e d)", e=2),
                     in_=o_t[:, hs].rearrange("p h e d -> p h (e d)"),
                 )
 
@@ -204,8 +219,14 @@ def tile_multiheadattention_pa_kernel(tc, hidden_states, Wq_words, Wq_scales, Wk
             for b in range(2):
                 project(mat, blk, 2 * b)
                 project(mat, blk, 2 * b + 1)
-                finish(mat, blk, b, nc.gpsimd)
-        for t in range(4):
-            project(1, 3, t)
-        finish(1, 3, 0, nc.vector)
-        finish(1, 3, 1, nc.vector, pieces=2)
+                if c < 6 or b == 0:
+                    finish(mat, blk, b, nc.gpsimd)
+        late = p_tiles[1]
+        with tc.manual_schedule(engines={mybir.EngineType.PE}):
+            project(1, 3, 0)
+            project(1, 3, 1)
+            finish(1, 3, 0, nc.gpsimd, pieces=2, queue=nc.sync)
+            project(1, 3, 2)
+            project(1, 3, 3)
+            finish_on_tensor(1, 2, 1, late)
+            finish(1, 3, 1, nc.vector, pieces=2, queue=nc.sync)

@@ -52,7 +52,7 @@ def tile_multiheadattention_pa_kernel(tc, hidden_states, Wq_words, Wq_scales, Wk
         words = {}
         planes = {}
 
-        def load_w(i):
+        def load_w(i, pieces=1):
             mat, first, count = W_LOADS[i]
             wt = keep.tile([P, PASSES, 1024 * count], U8, name="w%d" % i, align_bytes=64)
             pl = keep.tile([P, PASSES, 512 * count], U8, name="s%d" % i, align_bytes=64)
@@ -64,10 +64,12 @@ def tile_multiheadattention_pa_kernel(tc, hidden_states, Wq_words, Wq_scales, Wk
                     out=pl[32 * q:32 * q + 4, :, :].bitcast(I32),
                     in_=w_scales[mat][:, 4 * q:4 * q + 4, c0:c1].rearrange("g r n -> r g n").bitcast(I32),
                 )
-            nc.sync.dma_start(
-                out=wt[:].bitcast(I32),
-                in_=w_words[mat][:, :, 2 * c0:2 * c1].rearrange("g p n -> p g n").bitcast(I32),
-            )
+            step = PASSES // pieces
+            for g0 in range(0, PASSES, step):
+                nc.sync.dma_start(
+                    out=wt[:, g0:g0 + step, :].bitcast(I32),
+                    in_=w_words[mat][g0:g0 + step, :, 2 * c0:2 * c1].rearrange("g p n -> p g n").bitcast(I32),
+                )
             for j in range(count):
                 words[(mat, first + j)] = (wt, j)
                 planes[(mat, first + j)] = (pl, j)
@@ -92,8 +94,8 @@ def tile_multiheadattention_pa_kernel(tc, hidden_states, Wq_words, Wq_scales, Wk
         load_x(0, 2)
         load_x(1, 1)
         load_x(2, 1)
-        load_x(3, 1)
-        load_w(0)
+        load_x(3, 2)
+        load_w(0, 2)
 
         for s in range(6):
             w = 1 << s
@@ -171,11 +173,12 @@ def tile_multiheadattention_pa_kernel(tc, hidden_states, Wq_words, Wq_scales, Wk
                 op=ALU.mult,
             )
 
-        def finish(mat, blk, b, adder, pieces=1, queue=None):
+        def finish(mat, blk, b, adder, pieces=(4,), queue=None):
             o_t = work.tile([P, 4, 2, P], F32, name="o_t")
-            heads = 4 // pieces
-            for i in range(pieces):
-                hs = slice(heads * i, heads * (i + 1))
+            h1 = 0
+            for heads in pieces:
+                h0, h1 = h1, h1 + heads
+                hs = slice(h0, h1)
                 pv = p_tiles[b][:, hs].rearrange("p h e w (u j) -> p (h e w) u j", u=2)
                 adder.tensor_tensor(
                     out=o_t[:, hs].rearrange("p h e (w j) -> p (h e w) j", w=2),
@@ -184,22 +187,24 @@ def tile_multiheadattention_pa_kernel(tc, hidden_states, Wq_words, Wq_scales, Wk
                     op=ALU.add,
                 )
                 (queue or nc.scalar).dma_start(
-                    out=outs[mat][b, 4 * blk + heads * i:4 * blk + heads * (i + 1)].rearrange("h (m e) d -> m h (e d)", e=2),
+                    out=outs[mat][b, 4 * blk + h0:4 * blk + h1].rearrange("h (m e) d -> m h (e d)", e=2),
                     in_=o_t[:, hs].rearrange("p h e d -> p h (e d)"),
                 )
 
         def finish_on_tensor(mat, blk, b, prod):
             o_t = work.tile([P, 4, 2, P], F32, name="o_t")
             pv = prod[:].rearrange("p h e w (u j) -> p h e w u j", u=2)
-            for i in range(2):
-                hs = slice(2 * i, 2 * i + 2)
+            h1 = 0
+            for heads in (2, 1, 1):
+                h0, h1 = h1, h1 + heads
+                hs = slice(h0, h1)
                 total = psum.tile([P, 2, 2, P], F32, tag="bank", name="total")
                 for e in range(2):
                     for u in range(2):
-                        nc.tensor.matmul(out=total[:, e, :, :], lhsT=ident[:], rhs=pv[:, hs, e, :, u, :], start=(u == 0), stop=(u == 1))
-                nc.scalar.copy(out=o_t[:, hs, :, :], in_=total[:].rearrange("p e h d -> p h e d"))
+                        nc.tensor.matmul(out=total[:, e, 0:heads, :], lhsT=ident[:], rhs=pv[:, hs, e, :, u, :], start=(u == 0), stop=(u == 1))
+                nc.scalar.copy(out=o_t[:, hs, :, :], in_=total[:, :, 0:heads, :].rearrange("p e h d -> p h e d"))
                 nc.scalar.dma_start(
-                    out=outs[mat][b, 4 * blk + 2 * i:4 * blk + 2 * i + 2].rearrange("h (m e) d -> m h (e d)", e=2),
+                    out=outs[mat][b, 4 * blk + h0:4 * blk + h1].rearrange("h (m e) d -> m h (e d)", e=2),
                     in_=o_t[:, hs].rearrange("p h e d -> p h (e d)"),
                 )
 
@@ -225,8 +230,8 @@ def tile_multiheadattention_pa_kernel(tc, hidden_states, Wq_words, Wq_scales, Wk
         with tc.manual_schedule(engines={mybir.EngineType.PE}):
             project(1, 3, 0)
             project(1, 3, 1)
-            finish(1, 3, 0, nc.gpsimd, pieces=2, queue=nc.sync)
+            finish(1, 3, 0, nc.gpsimd, pieces=(2, 2), queue=nc.sync)
             project(1, 3, 2)
             project(1, 3, 3)
             finish_on_tensor(1, 2, 1, late)
-            finish(1, 3, 1, nc.vector, pieces=2, queue=nc.sync)
+            finish(1, 3, 1, nc.vector, pieces=(2, 1, 1), queue=nc.sync)

@@ -92,7 +92,7 @@ def tile_multiheadattention_pa_kernel(tc, hidden_states, Wq_words, Wq_scales, Wk
         nc.scalar.activation(out=warm[:], in_=warm[:], func=ACT.Sin)
 
         load_x(0, 2)
-        load_x(1, 1)
+        load_x(1, 2)
         load_x(2, 1)
         load_x(3, 2)
         load_w(0, 2)

@@ -173,9 +173,9 @@ def tile_multiheadattention_pa_kernel(tc, hidden_states, Wq_words, Wq_scales, Wk
                 op=ALU.mult,
             )
 
-        def finish(mat, blk, b, adder, pieces=(4,), queue=None):
-            o_t = work.tile([P, 4, 2, P], F32, name="o_t")
-            h1 = 0
+        def finish(mat, blk, b, adder, pieces=(4,), queue=None, o_t=None, h1=0):
+            if o_t is None:
+                o_t = work.tile([P, 4, 2, P], F32, name="o_t")
             for heads in pieces:
                 h0, h1 = h1, h1 + heads
                 hs = slice(h0, h1)
@@ -191,11 +191,10 @@ def tile_multiheadattention_pa_kernel(tc, hidden_states, Wq_words, Wq_scales, Wk
                     in_=o_t[:, hs].rearrange("p h e d -> p h (e d)"),
                 )
 
-        def finish_on_tensor(mat, blk, b, prod):
-            o_t = work.tile([P, 4, 2, P], F32, name="o_t")
+        def finish_on_tensor(mat, blk, b, prod, o_t, pieces):
             pv = prod[:].rearrange("p h e w (u j) -> p h e w u j", u=2)
             h1 = 0
-            for heads in (2, 1, 1):
+            for heads in pieces:
                 h0, h1 = h1, h1 + heads
                 hs = slice(h0, h1)
                 total = psum.tile([P, 2, 2, P], F32, tag="bank", name="total")
@@ -226,12 +225,17 @@ def tile_multiheadattention_pa_kernel(tc, hidden_states, Wq_words, Wq_scales, Wk
                 project(mat, blk, 2 * b + 1)
                 if c < 6 or b == 0:
                     finish(mat, blk, b, nc.gpsimd)
-        late = p_tiles[1]
+        late_a = p_tiles[1]
+        out_a = work.tile([P, 4, 2, P], F32, name="o_t")
+        finish(1, 2, 1, nc.gpsimd, pieces=(2,), queue=nc.sync, o_t=out_a, h1=2)
         with tc.manual_schedule(engines={mybir.EngineType.PE}):
             project(1, 3, 0)
             project(1, 3, 1)
-            finish(1, 3, 0, nc.gpsimd, pieces=(2, 2), queue=nc.sync)
+            late_b = p_tiles[0]
+            out_b = work.tile([P, 4, 2, P], F32, name="o_t")
+            finish(1, 3, 0, nc.gpsimd, pieces=(2,), queue=nc.sync, o_t=out_b, h1=2)
             project(1, 3, 2)
             project(1, 3, 3)
-            finish_on_tensor(1, 2, 1, late)
+            finish_on_tensor(1, 2, 1, late_a, out_a, (2,))
+            finish_on_tensor(1, 3, 0, late_b, out_b, (1, 1))
             finish(1, 3, 1, nc.vector, pieces=(2, 1, 1), queue=nc.sync)

from contextlib import ExitStack
import math

import concourse.mybir as mybir
from concourse.masks import make_identity

F32 = mybir.dt.float32
BF16 = mybir.dt.bfloat16
I32 = mybir.dt.int32
U32 = mybir.dt.uint32
U8 = mybir.dt.uint8
E5X4 = mybir.dt.float8_e5m2_x4
E2X4 = mybir.dt.float4_e2m1fn_x4
ALU = mybir.AluOpType
ACT = mybir.ActivationFunctionType

FLOPS = 2 * 512 * 2048 * 4096

P = 128
PASSES = 4
RATIO = 10000.0 ** (-1.0 / 64.0)
TWO_PI_HI = 6.28125
TWO_PI_LO = 2.0 * math.pi - TWO_PI_HI
W_LOADS = ((0, 0, 1), (0, 1, 1), (0, 2, 2), (1, 0, 2), (1, 2, 2))


def tile_multiheadattention_pa_kernel(tc, hidden_states, Wq_words, Wq_scales, Wk_words, Wk_scales, out_0, out_1):
    nc = tc.nc
    w_words = (Wq_words, Wk_words)
    w_scales = (Wq_scales, Wk_scales)
    outs = (out_0, out_1)

    with ExitStack() as ctx:
        keep = ctx.enter_context(tc.tile_pool(name="keep", bufs=1))
        work = ctx.enter_context(tc.tile_pool(name="work", bufs=5))
        products = ctx.enter_context(tc.tile_pool(name="products", bufs=12))
        psum = ctx.enter_context(tc.psum_pool(name="psum", bufs=7))
        psum_idle = ctx.enter_context(tc.psum_pool(name="psum_idle", bufs=1))

        x_sb = []
        for t in range(4):
            x_t = keep.tile([P, 2048], BF16, name="x%d" % t)
            x_sb.append(x_t)

        def load_x(t, pieces):
            b, e = divmod(t, 2)
            src = hidden_states[b].rearrange("(m e) k -> m e k", e=2)
            step = 2048 // pieces
            for i in range(pieces):
                nc.sync.dma_start(out=x_sb[t][:, i * step:(i + 1) * step], in_=src[:, e, i * step:(i + 1) * step])

        words = {}
        planes = {}

        def load_w(i, pieces=1):
            mat, first, count = W_LOADS[i]
            wt = keep.tile([P, PASSES, 1024 * count], U8, name="w%d" % i, align_bytes=64)
            pl = keep.tile([P, PASSES, 512 * count], U8, name="s%d" % i, align_bytes=64)
            nc.vector.memset(pl[:].bitcast(I32), 0)
            c0 = 512 * first
            c1 = c0 + 512 * count
            for q in range(4):
                nc.sync.dma_start(
                    out=pl[32 * q:32 * q + 4, :, :].bitcast(I32),
                    in_=w_scales[mat][:, 4 * q:4 * q + 4, c0:c1].rearrange("g r n -> r g n").bitcast(I32),
                )
            step = PASSES // pieces
            for g0 in range(0, PASSES, step):
                nc.sync.dma_start(
                    out=wt[:, g0:g0 + step, :].bitcast(I32),
                    in_=w_words[mat][g0:g0 + step, :, 2 * c0:2 * c1].rearrange("g p n -> p g n").bitcast(I32),
                )
            for j in range(count):
                words[(mat, first + j)] = (wt, j)
                planes[(mat, first + j)] = (pl, j)

        zeros = keep.tile([P, 512], BF16, name="zeros")
        nc.gpsimd.memset(zeros[:], 0.0)
        idle_bank = psum_idle.tile([P, 512], F32, name="idle_bank")

        def keep_clock(count):
            for i in range(count):
                nc.tensor.matmul(out=idle_bank[:], lhsT=zeros[:, 0:P], rhs=zeros[:], start=True, stop=True)

        ang = keep.tile([P, 2, 64], F32, name="ang")
        nc.gpsimd.iota(ang[:, :, 0:1], pattern=[[1, 2]], base=0, channel_multiplier=2, allow_small_or_imprecise_dtypes=True)
        ident = keep.tile([P, P], F32, name="ident")
        make_identity(nc, ident[:])

        warm = keep.tile([P, 1], F32, name="warm")
        nc.vector.memset(warm[:], 0.0)
        nc.scalar.activation(out=warm[:], in_=warm[:], func=ACT.Sin)

        load_x(0, 2)
        load_x(1, 2)
        load_x(2, 1)
        load_x(3, 2)
        load_w(0, 2)

        for s in range(6):
            w = 1 << s
            nc.vector.tensor_scalar(out=ang[:, :, w:2 * w], in0=ang[:, :, 0:w], scalar1=RATIO ** w, scalar2=None, op0=ALU.mult)
        turns = keep.tile([P, 2, 64], I32, name="turns")
        nc.vector.tensor_scalar(out=turns[:], in0=ang[:], scalar1=1.0 / (2.0 * math.pi), scalar2=None, op0=ALU.mult)
        red1 = keep.tile([P, 2, 64], F32, name="red1")
        nc.vector.scalar_tensor_tensor(out=red1[:], in0=turns[:], scalar=-TWO_PI_HI, in1=ang[:], op0=ALU.mult, op1=ALU.add)
        red = keep.tile([P, 2, 64], F32, name="red")
        nc.vector.scalar_tensor_tensor(out=red[:], in0=turns[:], scalar=-TWO_PI_LO, in1=red1[:], op0=ALU.mult, op1=ALU.add)
        absred = keep.tile([P, 2, 64], F32, name="absred")
        nc.vector.scalar_tensor_tensor(out=absred[:], in0=red[:], scalar=-1.0, in1=red[:], op0=ALU.mult, op1=ALU.max)

        tab = keep.tile([P, 2, 256], F32, name="tab")
        tab_k = tab[:].rearrange("p e (k j) -> p e k j", k=4)
        nc.scalar.activation(out=tab_k[:, :, 2, :], in_=red[:], func=ACT.Sin)
        nc.scalar.activation(out=tab_k[:, :, 1, :], in_=red[:], func=ACT.Sin, scale=-1.0)
        nc.scalar.activation(out=tab_k[:, :, 0:4:3, :], in_=absred[:].unsqueeze(2).to_broadcast([P, 2, 2, 64]), func=ACT.Sin, scale=-1.0, bias=0.5 * math.pi)

        for i in range(1, len(W_LOADS)):
            load_w(i)

        codes = []
        x_scales = []
        grouped = []
        for t in range(4):
            c_t = keep.tile([P, PASSES, P], U32, name="codes%d" % t, align_bytes=64)
            s_t = keep.tile([P, PASSES, P], U8, name="xs%d" % t, align_bytes=64)
            g_t = keep.tile([P, PASSES, P, 4], BF16, name="grp%d" % t, align_bytes=64)
            codes.append(c_t)
            x_scales.append(s_t)
            grouped.append(g_t)

        def prepare_x(t):
            x_words = x_sb[t][:].bitcast(F32)
            g32 = grouped[t][:].rearrange("p g r t -> p g (r t)").bitcast(F32).rearrange("p g (r u) -> p g r u", u=2)
            for hb in range(2):
                xt = psum.tile([P, 2, 2, P], F32, tag="bank", name="xt")
                for gi in range(2):
                    g = 2 * hb + gi
                    for u in range(2):
                        nc.tensor.transpose(xt[:, gi, u, :], x_words[:, 256 * g + u:256 * (g + 1):2], ident[:])
                nc.scalar.copy(out=g32[:, 2 * hb:2 * hb + 2, :, :], in_=xt[:].rearrange("p g u r -> p g r u"))
                nc.vector.quantize_mx(
                    out=codes[t][:, 2 * hb:2 * hb + 2, :].rearrange("p g m -> p (g m)").bitcast(E5X4),
                    scales=x_scales[t][:, 2 * hb:2 * hb + 2, :].rearrange("p g m -> p (g m)"),
                    in_=grouped[t][:, 2 * hb:2 * hb + 2, :, :].rearrange("p g r t -> p (g r t)"),
                )

        p_tiles = {}

        def project(mat, blk, t):
            b, e = divmod(t, 2)
            wt, j = words[(mat, blk)]
            pl, j = planes[(mat, blk)]
            acc = psum.tile([P, 512], F32, tag="bank", name="acc")
            for g in range(PASSES):
                nc.tensor.matmul_mx(
                    out=acc[:],
                    lhsT=codes[t][:, g, :].bitcast(E5X4),
                    lhsT_scale=x_scales[t][:, g, :],
                    rhs=wt[:, g, 1024 * j:1024 * (j + 1)].bitcast(E2X4),
                    rhs_scale=pl[:, g, 512 * j:512 * (j + 1)],
                    start=(g == 0),
                    stop=(g == PASSES - 1),
                )
            if e == 0:
                p_new = products.tile([P, 4, 2, 2, P], F32, name="p_new")
                p_tiles[b] = p_new
            prod = p_tiles[b]
            nc.vector.tensor_tensor(
                out=prod[:, :, e, :, :].rearrange("p h w d -> p w h d"),
                in0=acc[:].rearrange("p (h d) -> p h d", h=4).unsqueeze(1).to_broadcast([P, 2, 4, P]),
                in1=tab[:, e, :].rearrange("p (w d) -> p w d", w=2).unsqueeze(2).to_broadcast([P, 2, 4, P]),
                op=ALU.mult,
            )

        def finish(mat, blk, b, adder, pieces=(4,), queue=None, o_t=None, h1=0):
            if o_t is None:
                o_t = work.tile([P, 4, 2, P], F32, name="o_t")
            for heads in pieces:
                h0, h1 = h1, h1 + heads
                hs = slice(h0, h1)
                pv = p_tiles[b][:, hs].rearrange("p h e w (u j) -> p (h e w) u j", u=2)
                adder.tensor_tensor(
                    out=o_t[:, hs].rearrange("p h e (w j) -> p (h e w) j", w=2),
                    in0=pv[:, :, 0, :],
                    in1=pv[:, :, 1, :],
                    op=ALU.add,
                )
                (queue or nc.scalar).dma_start(
                    out=outs[mat][b, 4 * blk + h0:4 * blk + h1].rearrange("h (m e) d -> m h (e d)", e=2),
                    in_=o_t[:, hs].rearrange("p h e d -> p h (e d)"),
                )

        def finish_on_tensor(mat, blk, b, prod, o_t, pieces):
            pv = prod[:].rearrange("p h e w (u j) -> p h e w u j", u=2)
            h1 = 0
            for heads in pieces:
                h0, h1 = h1, h1 + heads
                hs = slice(h0, h1)
                total = psum.tile([P, 2, 2, P], F32, tag="bank", name="total")
                for e in range(2):
                    for u in range(2):
                        nc.tensor.matmul(out=total[:, e, 0:heads, :], lhsT=ident[:], rhs=pv[:, hs, e, :, u, :], start=(u == 0), stop=(u == 1))
                nc.scalar.copy(out=o_t[:, hs, :, :], in_=total[:, :, 0:heads, :].rearrange("p e h d -> p h e d"))
                nc.scalar.dma_start(
                    out=outs[mat][b, 4 * blk + h0:4 * blk + h1].rearrange("h (m e) d -> m h (e d)", e=2),
                    in_=o_t[:, hs].rearrange("p h e d -> p h (e d)"),
                )

        with tc.manual_schedule(engines={mybir.EngineType.PE}):
            keep_clock(3)
            prepare_x(0)
            prepare_x(1)
            keep_clock(2)
            prepare_x(2)
            prepare_x(3)
            for b in range(2):
                project(0, 0, 2 * b)
                project(0, 0, 2 * b + 1)
                finish(0, 0, b, nc.gpsimd)
        for c in range(1, 7):
            mat, blk = divmod(c, 4)
            for b in range(2):
                project(mat, blk, 2 * b)
                project(mat, blk, 2 * b + 1)
                if c < 6 or b == 0:
                    finish(mat, blk, b, nc.gpsimd)
        late_a = p_tiles[1]
        out_a = work.tile([P, 4, 2, P], F32, name="o_t")
        finish(1, 2, 1, nc.gpsimd, pieces=(2,), queue=nc.sync, o_t=out_a, h1=2)
        with tc.manual_schedule(engines={mybir.EngineType.PE}):
            project(1, 3, 0)
            project(1, 3, 1)
            late_b = p_tiles[0]
            out_b = work.tile([P, 4, 2, P], F32, name="o_t")
            finish(1, 3, 0, nc.gpsimd, pieces=(2,), queue=nc.sync, o_t=out_b, h1=2)
            project(1, 3, 2)
            project(1, 3, 3)
            finish_on_tensor(1, 2, 1, late_a, out_a, (2,))
            finish_on_tensor(1, 3, 0, late_b, out_b, (1, 1))
            finish(1, 3, 1, nc.vector, pieces=(2, 1, 1), queue=nc.sync)
